import numpy as np
import ml_dtypes


def mxq(x, axis, fmt="e4m3"):
    dtype, down = {"e4m3": (ml_dtypes.float8_e4m3fn, 7), "e5m2": (ml_dtypes.float8_e5m2, 14)}[fmt]
    v = np.moveaxis(np.asarray(x, np.float32).astype(ml_dtypes.bfloat16).astype(np.float64), axis, -1)
    blocks = v.reshape(v.shape[:-1] + (-1, 32))
    amax = np.abs(blocks).max(-1, keepdims=True)
    byte = np.maximum(np.where(amax > 0, np.frexp(amax)[1] - 1 + 127, 0) - down, 1)
    scale = np.exp2(byte - 127.0)
    codes = (blocks / scale).astype(np.float32).astype(dtype).astype(np.float64)
    return np.moveaxis((codes * scale).reshape(v.shape), -1, axis)


WIDE = False


def mx_kscale(k):
    if not WIDE:
        return np.ones(k)
    levels = np.array([18, -18])
    if k % 512:
        return np.exp2(np.random.permutation(np.resize(levels, k // 32))).repeat(32)
    a = np.empty((k // 512, 16))
    for p in range(k // 512):
        a[p, :8] = np.random.permutation(np.resize(levels, 8))
        for g in range(8):
            far = levels[np.abs(levels - a[p, g]) >= 10]
            a[p, g + 8] = far[np.random.randint(len(far))]
    return np.exp2(a.ravel()).repeat(32)


BF16 = ml_dtypes.bfloat16


def bf(x):
    return np.asarray(x, np.float32).astype(BF16)


def f64(x):
    return np.asarray(x).astype(np.float64)


M, K, N, D = 1024, 1536, 1024, 1024
GAMMA, ALPHA = 0.5, 0.1


def setup_inputs():
    s = mx_kscale(M)
    u = mx_kscale(D)
    m = np.maximum(s, 1.0)[:, None]
    support0 = bf(np.random.standard_normal((M, K)) / np.sqrt(K))
    f = bf(1.0 + 0.1 * np.random.standard_normal(K))
    support1 = bf(np.random.standard_normal((K, N)) / np.sqrt(N))
    adj0 = bf(np.random.standard_normal((M, N)) / np.sqrt(N))
    x0 = bf(np.random.standard_normal((N, D)))
    h0 = bf(np.random.standard_normal((M, D)))
    go = bf(4.0 * np.random.standard_normal((M, D)) * np.exp2(np.random.randint(-6, 1, (M, 1))) / m * u)
    p = (f64(support0) * f64(f)[None, :]) @ f64(support1)
    return {"support0": support0, "f": f, "support1": support1,
            "adj": bf(f64(adj0) * m), "x": bf(f64(x0) / u), "h0": h0,
            "p": np.asarray(p, np.float32), "grad_out": go}


def reference(support0, f, support1, adj, x, h0, p, grad_out):
    dz = (1.0 - ALPHA) * f64(grad_out)
    blend = GAMMA * f64(p) + (1.0 - GAMMA) * f64(adj)
    dx = mxq(blend, 0, "e4m3").T @ mxq(dz, 0, "e5m2")
    dblend = mxq(dz, 1, "e5m2") @ mxq(f64(x), 1, "e4m3").T
    return dx, (1.0 - GAMMA) * dblend

@@ -1,0 +1,210 @@
+from contextlib import ExitStack
+
+import concourse.mybir as mybir
+from concourse.masks import make_identity
+
+M, N, D = 1024, 1024, 1024
+FLOPS = 2 * 2 * M * N * D
+BYTES = M * N * (4 + 2) + N * D * 2 + M * D * 2 + N * D * 4 + M * N * 4
+
+F32 = mybir.dt.float32
+BF16 = mybir.dt.bfloat16
+U32 = mybir.dt.uint32
+U8 = mybir.dt.uint8
+E4M3 = mybir.dt.float8_e4m3fn_x4
+E5M2 = mybir.dt.float8_e5m2_x4
+COPY = mybir.ActivationFunctionType.Copy
+MULT = mybir.AluOpType.mult
+ADD = mybir.AluOpType.add
+
+P = 128
+PACK = 4
+K_PASS = P * PACK
+BANK = 512
+RUN = 4
+BLEND_COLS = 256
+DZ_FACTOR = 0.9
+HALF = 0.5
+
+
+def tile_combinelayer_pa_v_kernel(tc, support0, f, support1, adj, x, h0, p, grad_out, out_0, out_1):
+    nc = tc.nc
+    with ExitStack() as ctx:
+        keep = ctx.enter_context(tc.tile_pool(name="keep", bufs=1))
+        stage = ctx.enter_context(tc.tile_pool(name="stage", bufs=8))
+        sums = ctx.enter_context(tc.tile_pool(name="sums", bufs=4))
+        results = ctx.enter_context(tc.tile_pool(name="results", bufs=8))
+        banks = ctx.enter_context(tc.psum_pool(name="banks", bufs=8))
+        ctx.enter_context(tc.manual_schedule())
+
+        def load(src, g, dtype, name):
+            rows = keep.tile([P, PACK, src.shape[1]], dtype, name=name, align_bytes=64)
+            nc.sync.dma_start(
+                out=rows[:], in_=src[g * K_PASS : (g + 1) * K_PASS, :].rearrange("(p j) w -> p j w", j=PACK)
+            )
+            return rows
+
+        go_rows, x_rows, adj_rows, p_rows = [], [], [], []
+        for g in range(2):
+            go_rows.append(load(grad_out, g, BF16, "go%d" % g))
+            x_rows.append(load(x, g, BF16, "x%d" % g))
+        for g in range(2):
+            adj_rows.append(load(adj, g, BF16, "adj%d" % g))
+            p_rows.append(load(p, g, F32, "p%d" % g))
+
+        ident = keep.tile([P, P], F32, name="ident")
+        make_identity(nc, ident[:])
+        warm = keep.tile([P, 1], F32, name="warm")
+        nc.scalar.activation(out=warm[:], in_=ident[:, 0:1], func=COPY, scale=HALF)
+
+        def quantize(grouped, fmt, name):
+            width = grouped.shape[1] // PACK
+            codes = keep.tile([P, width], U32, name=name + "_codes", align_bytes=64)
+            scales = keep.tile([P, width], U8, name=name + "_scales", align_bytes=64)
+            nc.vector.quantize_mx(out=codes[:].bitcast(fmt), scales=scales[:], in_=grouped[:])
+            return codes, scales, fmt
+
+        def turn(rows, empty):
+            words = rows[:].bitcast(F32)
+            turned = []
+            for h in range(2):
+                grouped = stage.tile([P, K_PASS * PACK], BF16, name="grouped", align_bytes=64)
+                for pair in range(2):
+                    bank = banks.tile([P, 2, 2 * P], F32, name="bank")
+                    for b in range(2):
+                        for u in range(2):
+                            nc.tensor.transpose(
+                                bank[:, u, b * P : (b + 1) * P],
+                                words[:, 2 * pair + b, 256 * h + u : 256 * (h + 1) : 2],
+                                ident[:],
+                            )
+                    empty(grouped[:, pair * 1024 : (pair + 1) * 1024], bank)
+                turned.append(grouped)
+            return turned
+
+        def empty_x(dst, bank):
+            nc.scalar.copy(
+                out=dst.bitcast(F32).rearrange("q (c u) -> q c u", u=2), in_=bank[:].rearrange("q u c -> q c u")
+            )
+
+        def empty_dz(dst, bank):
+            nc.vector.tensor_scalar(
+                out=dst.rearrange("q (c u e) -> q c u e", u=2, e=2),
+                in0=bank[:].bitcast(BF16).rearrange("q u (c e) -> q c u e", e=2),
+                scalar1=DZ_FACTOR,
+                scalar2=None,
+                op0=MULT,
+            )
+
+        def by_runs(rows, cols):
+            return rows[:, :, cols].rearrange("p j (c i) -> p c j i", i=RUN)
+
+        def woven(tile):
+            return tile[:].rearrange("p (c i j) -> p c j i", i=RUN, j=PACK)
+
+        def weave_dz(g, half, on_scalar):
+            grouped = stage.tile([P, K_PASS * PACK], BF16, name="grouped", align_bytes=64)
+            src = by_runs(go_rows[g], slice(half * BANK, (half + 1) * BANK))
+            if on_scalar:
+                nc.scalar.activation(out=woven(grouped), in_=src, func=COPY, scale=DZ_FACTOR)
+            else:
+                nc.vector.tensor_scalar(out=woven(grouped), in0=src, scalar1=DZ_FACTOR, scalar2=None, op0=MULT)
+            return grouped
+
+        def weave_sum(g, part):
+            cols = slice(part * BLEND_COLS, (part + 1) * BLEND_COLS)
+            total = sums.tile([P, BLEND_COLS * PACK], BF16, name="total", align_bytes=64)
+            nc.vector.tensor_tensor(
+                out=woven(total), in0=by_runs(p_rows[g], cols), in1=by_runs(adj_rows[g], cols), op=ADD
+            )
+            return total
+
+        def one_pass(acc, stationary, first, moving, k):
+            cols = slice(first, first + P)
+            s_codes, s_scales, s_fmt = stationary[k]
+            m_codes, m_scales, m_fmt = moving[k]
+            nc.tensor.matmul_mx(
+                out=acc[:],
+                lhsT=s_codes[:, cols].bitcast(s_fmt),
+                lhsT_scale=s_scales[:, cols],
+                rhs=m_codes[:].bitcast(m_fmt),
+                rhs_scale=m_scales[:],
+                start=(k == 0),
+                stop=(k == 1),
+            )
+
+        dblend = {}
+
+        def out1_block(g, half):
+            for j in range(PACK):
+                acc = banks.tile([P, BANK], F32, name="bank")
+                for h in range(2):
+                    one_pass(acc, dz_t[g], j * P, x_t[half], h)
+                if (g, j // 2) not in dblend:
+                    dblend[(g, j // 2)] = results.tile([P, 2, N], F32, name="result")
+                dst = dblend[(g, j // 2)][:, j % 2, half * BANK : (half + 1) * BANK]
+                nc.scalar.activation(
+                    out=dst.rearrange("m (p j) -> m p j", j=PACK),
+                    in_=acc[:].rearrange("m (j p) -> m p j", j=PACK),
+                    func=COPY,
+                    scale=HALF,
+                )
+                if half == 1 and j % 2 == 1:
+                    rows = out_1[g * K_PASS : (g + 1) * K_PASS, :].rearrange("(p j) n -> p j n", j=PACK)
+                    nc.sync.dma_start(out=rows[:, j - 1 : j + 1, :], in_=dblend[(g, j // 2)][:])
+
+        dz_t, x_t = [], []
+        dz_m = [[], []]
+        w00 = weave_dz(0, 0, True)
+        t = turn(go_rows[0], empty_dz)
+        w01 = weave_dz(0, 1, False)
+        dz_t.append([quantize(t[h], E5M2, "dzt0%d" % h) for h in range(2)])
+        t = turn(x_rows[0], empty_x)
+        dz_m[0].append(quantize(w00, E5M2, "dzm00"))
+        x_t.append([quantize(t[h], E4M3, "xt0%d" % h) for h in range(2)])
+        w10 = weave_dz(1, 0, True)
+        t = turn(go_rows[1], empty_dz)
+        dz_m[1].append(quantize(w01, E5M2, "dzm01"))
+        dz_t.append([quantize(t[h], E5M2, "dzt1%d" % h) for h in range(2)])
+        out1_block(0, 0)
+        t = turn(x_rows[1], empty_x)
+        w11 = weave_dz(1, 1, False)
+        x_t.append([quantize(t[h], E4M3, "xt1%d" % h) for h in range(2)])
+        dz_m[0].append(quantize(w10, E5M2, "dzm10"))
+        dz_m[1].append(quantize(w11, E5M2, "dzm11"))
+        out1_block(1, 0)
+        out1_block(0, 1)
+        out1_block(1, 1)
+
+        parts = N // BLEND_COLS
+        steps = [(g, part) for g in range(2) for part in range(parts)]
+        blend = [[] for part in range(parts)]
+        groups = [(b, half) for b in range(2) for half in range(2)]
+        open_sums = {}
+
+        def open_part(part):
+            for b, half in groups:
+                open_sums[(part, b, half)] = banks.tile([P, BANK], F32, name="bank")
+                one_pass(open_sums[(part, b, half)], blend[part], b * P, dz_m[half], 0)
+
+        def close_part(part):
+            dx = results.tile([P, 2, D], F32, name="result")
+            for b, half in groups:
+                acc = open_sums[(part, b, half)]
+                one_pass(acc, blend[part], b * P, dz_m[half], 1)
+                nc.scalar.activation(out=dx[:, b, half * BANK : (half + 1) * BANK], in_=acc[:], func=COPY, scale=HALF)
+            rows = out_0[part * BLEND_COLS : (part + 1) * BLEND_COLS, :]
+            nc.sync.dma_start(out=rows.rearrange("(b p) d -> p b d", p=P), in_=dx[:])
+
+        waiting = weave_sum(*steps[0])
+        for s, (g, part) in enumerate(steps):
+            ready = waiting
+            if s + 1 < len(steps):
+                waiting = weave_sum(*steps[s + 1])
+            blend[part].append(quantize(ready, E4M3, "blend%d%d" % (g, part)))
+            if g == 0 and part < 2:
+                open_part(part)
+            if g == 1:
+                close_part(part)
+                if part + 2 < parts:
+                    open_part(part + 2)

@@ -37,20 +37,21 @@ def tile_combinelayer_pa_v_kernel(tc, support0, f, support1, adj, x, h0, p, grad
         banks = ctx.enter_context(tc.psum_pool(name="banks", bufs=8))
         ctx.enter_context(tc.manual_schedule())
 
-        def load(src, g, dtype, name):
-            rows = keep.tile([P, PACK, src.shape[1]], dtype, name=name, align_bytes=64)
-            nc.sync.dma_start(
-                out=rows[:], in_=src[g * K_PASS : (g + 1) * K_PASS, :].rearrange("(p j) w -> p j w", j=PACK)
-            )
+        def load(src, g, dtype, name, first=0, width=1024):
+            rows = keep.tile([P, PACK, width], dtype, name=name, align_bytes=64)
+            part = src[g * K_PASS : (g + 1) * K_PASS, first : first + width]
+            nc.sync.dma_start(out=rows[:], in_=part.rearrange("(p j) w -> p j w", j=PACK))
             return rows
 
-        go_rows, x_rows, adj_rows, p_rows = [], [], [], []
+        go_rows, x_rows, adj_rows, p_rows = [], [], [], {}
         for g in range(2):
             go_rows.append(load(grad_out, g, BF16, "go%d" % g))
             x_rows.append(load(x, g, BF16, "x%d" % g))
         for g in range(2):
             adj_rows.append(load(adj, g, BF16, "adj%d" % g))
-            p_rows.append(load(p, g, F32, "p%d" % g))
+            p_rows[(g, 0)] = load(p, g, F32, "p%d0" % g, 0, BANK)
+        for g in range(2):
+            p_rows[(g, 1)] = load(p, g, F32, "p%d1" % g, BANK, BANK)
 
         ident = keep.tile([P, P], F32, name="ident")
         make_identity(nc, ident[:])
@@ -113,9 +114,10 @@ def tile_combinelayer_pa_v_kernel(tc, support0, f, support1, adj, x, h0, p, grad
 
         def weave_sum(g, part):
             cols = slice(part * BLEND_COLS, (part + 1) * BLEND_COLS)
+            p_cols = slice(part % 2 * BLEND_COLS, (part % 2 + 1) * BLEND_COLS)
             total = sums.tile([P, BLEND_COLS * PACK], BF16, name="total", align_bytes=64)
             nc.vector.tensor_tensor(
-                out=woven(total), in0=by_runs(p_rows[g], cols), in1=by_runs(adj_rows[g], cols), op=ADD
+                out=woven(total), in0=by_runs(p_rows[(g, part // 2)], p_cols), in1=by_runs(adj_rows[g], cols), op=ADD
             )
             return total
 
@@ -157,27 +159,27 @@ def tile_combinelayer_pa_v_kernel(tc, support0, f, support1, adj, x, h0, p, grad
         dz_m = [[], []]
         w00 = weave_dz(0, 0, True)
         t = turn(go_rows[0], empty_dz)
-        w01 = weave_dz(0, 1, False)
         dz_t.append([quantize(t[h], E5M2, "dzt0%d" % h) for h in range(2)])
+        w01 = weave_dz(0, 1, False)
         t = turn(x_rows[0], empty_x)
-        dz_m[0].append(quantize(w00, E5M2, "dzm00"))
         x_t.append([quantize(t[h], E4M3, "xt0%d" % h) for h in range(2)])
         w10 = weave_dz(1, 0, True)
         t = turn(go_rows[1], empty_dz)
-        dz_m[1].append(quantize(w01, E5M2, "dzm01"))
         dz_t.append([quantize(t[h], E5M2, "dzt1%d" % h) for h in range(2)])
-        out1_block(0, 0)
         t = turn(x_rows[1], empty_x)
-        w11 = weave_dz(1, 1, False)
+        w11 = weave_dz(1, 1, True)
+        dz_m[0].append(quantize(w00, E5M2, "dzm00"))
+        dz_m[1].append(quantize(w01, E5M2, "dzm01"))
         x_t.append([quantize(t[h], E4M3, "xt1%d" % h) for h in range(2)])
         dz_m[0].append(quantize(w10, E5M2, "dzm10"))
         dz_m[1].append(quantize(w11, E5M2, "dzm11"))
+        out1_block(0, 0)
         out1_block(1, 0)
         out1_block(0, 1)
         out1_block(1, 1)
 
         parts = N // BLEND_COLS
-        steps = [(g, part) for g in range(2) for part in range(parts)]
+        steps = [(g, part) for part in range(parts) for g in range(2)]
         blend = [[] for part in range(parts)]
         groups = [(b, half) for b in range(2) for half in range(2)]
         open_sums = {}
@@ -192,7 +194,11 @@ def tile_combinelayer_pa_v_kernel(tc, support0, f, support1, adj, x, h0, p, grad
             for b, half in groups:
                 acc = open_sums[(part, b, half)]
                 one_pass(acc, blend[part], b * P, dz_m[half], 1)
-                nc.scalar.activation(out=dx[:, b, half * BANK : (half + 1) * BANK], in_=acc[:], func=COPY, scale=HALF)
+                dst = dx[:, b, half * BANK : (half + 1) * BANK]
+                if part == parts - 1 and half == 1:
+                    nc.vector.tensor_scalar(out=dst, in0=acc[:], scalar1=HALF, scalar2=None, op0=MULT)
+                else:
+                    nc.scalar.activation(out=dst, in_=acc[:], func=COPY, scale=HALF)
             rows = out_0[part * BLEND_COLS : (part + 1) * BLEND_COLS, :]
             nc.sync.dma_start(out=rows.rearrange("(b p) d -> p b d", p=P), in_=dx[:])
 
@@ -202,9 +208,7 @@ def tile_combinelayer_pa_v_kernel(tc, support0, f, support1, adj, x, h0, p, grad
             if s + 1 < len(steps):
                 waiting = weave_sum(*steps[s + 1])
             blend[part].append(quantize(ready, E4M3, "blend%d%d" % (g, part)))
-            if g == 0 and part < 2:
+            if g == 0:
                 open_part(part)
-            if g == 1:
+            else:
                 close_part(part)
-                if part + 2 < parts:
-                    open_part(part + 2)

from contextlib import ExitStack

import concourse.mybir as mybir
from concourse.masks import make_identity

M, N, D = 1024, 1024, 1024
FLOPS = 2 * 2 * M * N * D
BYTES = M * N * (4 + 2) + N * D * 2 + M * D * 2 + N * D * 4 + M * N * 4

F32 = mybir.dt.float32
BF16 = mybir.dt.bfloat16
U32 = mybir.dt.uint32
U8 = mybir.dt.uint8
E4M3 = mybir.dt.float8_e4m3fn_x4
E5M2 = mybir.dt.float8_e5m2_x4
COPY = mybir.ActivationFunctionType.Copy
MULT = mybir.AluOpType.mult
ADD = mybir.AluOpType.add

P = 128
PACK = 4
K_PASS = P * PACK
BANK = 512
RUN = 4
BLEND_COLS = 256
DZ_FACTOR = 0.9
HALF = 0.5


def tile_combinelayer_pa_v_kernel(tc, support0, f, support1, adj, x, h0, p, grad_out, out_0, out_1):
    nc = tc.nc
    with ExitStack() as ctx:
        keep = ctx.enter_context(tc.tile_pool(name="keep", bufs=1))
        stage = ctx.enter_context(tc.tile_pool(name="stage", bufs=8))
        sums = ctx.enter_context(tc.tile_pool(name="sums", bufs=4))
        results = ctx.enter_context(tc.tile_pool(name="results", bufs=8))
        banks = ctx.enter_context(tc.psum_pool(name="banks", bufs=8))
        ctx.enter_context(tc.manual_schedule())

        def load(src, g, dtype, name, first=0, width=1024):
            rows = keep.tile([P, PACK, width], dtype, name=name, align_bytes=64)
            part = src[g * K_PASS : (g + 1) * K_PASS, first : first + width]
            nc.sync.dma_start(out=rows[:], in_=part.rearrange("(p j) w -> p j w", j=PACK))
            return rows

        go_rows, x_rows, adj_rows, p_rows = [], [], [], {}
        for g in range(2):
            go_rows.append(load(grad_out, g, BF16, "go%d" % g))
            x_rows.append(load(x, g, BF16, "x%d" % g))
        for g in range(2):
            adj_rows.append(load(adj, g, BF16, "adj%d" % g))
            p_rows[(g, 0)] = load(p, g, F32, "p%d0" % g, 0, BANK)
        for g in range(2):
            p_rows[(g, 1)] = load(p, g, F32, "p%d1" % g, BANK, BANK)

        ident = keep.tile([P, P], F32, name="ident")
        make_identity(nc, ident[:])
        warm = keep.tile([P, 1], F32, name="warm")
        nc.scalar.activation(out=warm[:], in_=ident[:, 0:1], func=COPY, scale=HALF)

        def quantize(grouped, fmt, name):
            width = grouped.shape[1] // PACK
            codes = keep.tile([P, width], U32, name=name + "_codes", align_bytes=64)
            scales = keep.tile([P, width], U8, name=name + "_scales", align_bytes=64)
            nc.vector.quantize_mx(out=codes[:].bitcast(fmt), scales=scales[:], in_=grouped[:])
            return codes, scales, fmt

        def turn(rows, empty):
            words = rows[:].bitcast(F32)
            turned = []
            for h in range(2):
                grouped = stage.tile([P, K_PASS * PACK], BF16, name="grouped", align_bytes=64)
                for pair in range(2):
                    bank = banks.tile([P, 2, 2 * P], F32, name="bank")
                    for b in range(2):
                        for u in range(2):
                            nc.tensor.transpose(
                                bank[:, u, b * P : (b + 1) * P],
                                words[:, 2 * pair + b, 256 * h + u : 256 * (h + 1) : 2],
                                ident[:],
                            )
                    empty(grouped[:, pair * 1024 : (pair + 1) * 1024], bank)
                turned.append(grouped)
            return turned

        def empty_x(dst, bank):
            nc.scalar.copy(
                out=dst.bitcast(F32).rearrange("q (c u) -> q c u", u=2), in_=bank[:].rearrange("q u c -> q c u")
            )

        def empty_dz(dst, bank):
            nc.vector.tensor_scalar(
                out=dst.rearrange("q (c u e) -> q c u e", u=2, e=2),
                in0=bank[:].bitcast(BF16).rearrange("q u (c e) -> q c u e", e=2),
                scalar1=DZ_FACTOR,
                scalar2=None,
                op0=MULT,
            )

        def by_runs(rows, cols):
            return rows[:, :, cols].rearrange("p j (c i) -> p c j i", i=RUN)

        def woven(tile):
            return tile[:].rearrange("p (c i j) -> p c j i", i=RUN, j=PACK)

        def weave_dz(g, half, on_scalar):
            grouped = stage.tile([P, K_PASS * PACK], BF16, name="grouped", align_bytes=64)
            src = by_runs(go_rows[g], slice(half * BANK, (half + 1) * BANK))
            if on_scalar:
                nc.scalar.activation(out=woven(grouped), in_=src, func=COPY, scale=DZ_FACTOR)
            else:
                nc.vector.tensor_scalar(out=woven(grouped), in0=src, scalar1=DZ_FACTOR, scalar2=None, op0=MULT)
            return grouped

        def weave_sum(g, part):
            cols = slice(part * BLEND_COLS, (part + 1) * BLEND_COLS)
            p_cols = slice(part % 2 * BLEND_COLS, (part % 2 + 1) * BLEND_COLS)
            total = sums.tile([P, BLEND_COLS * PACK], BF16, name="total", align_bytes=64)
            nc.vector.tensor_tensor(
                out=woven(total), in0=by_runs(p_rows[(g, part // 2)], p_cols), in1=by_runs(adj_rows[g], cols), op=ADD
            )
            return total

        def one_pass(acc, stationary, first, moving, k):
            cols = slice(first, first + P)
            s_codes, s_scales, s_fmt = stationary[k]
            m_codes, m_scales, m_fmt = moving[k]
            nc.tensor.matmul_mx(
                out=acc[:],
                lhsT=s_codes[:, cols].bitcast(s_fmt),
                lhsT_scale=s_scales[:, cols],
                rhs=m_codes[:].bitcast(m_fmt),
                rhs_scale=m_scales[:],
                start=(k == 0),
                stop=(k == 1),
            )

        dblend = {}

        def out1_block(g, half):
            for j in range(PACK):
                acc = banks.tile([P, BANK], F32, name="bank")
                for h in range(2):
                    one_pass(acc, dz_t[g], j * P, x_t[half], h)
                if (g, j // 2) not in dblend:
                    dblend[(g, j // 2)] = results.tile([P, 2, N], F32, name="result")
                dst = dblend[(g, j // 2)][:, j % 2, half * BANK : (half + 1) * BANK]
                nc.scalar.activation(
                    out=dst.rearrange("m (p j) -> m p j", j=PACK),
                    in_=acc[:].rearrange("m (j p) -> m p j", j=PACK),
                    func=COPY,
                    scale=HALF,
                )
                if half == 1 and j % 2 == 1:
                    rows = out_1[g * K_PASS : (g + 1) * K_PASS, :].rearrange("(p j) n -> p j n", j=PACK)
                    nc.sync.dma_start(out=rows[:, j - 1 : j + 1, :], in_=dblend[(g, j // 2)][:])

        dz_t, x_t = [], []
        dz_m = [[], []]
        w00 = weave_dz(0, 0, True)
        t = turn(go_rows[0], empty_dz)
        dz_t.append([quantize(t[h], E5M2, "dzt0%d" % h) for h in range(2)])
        w01 = weave_dz(0, 1, False)
        t = turn(x_rows[0], empty_x)
        x_t.append([quantize(t[h], E4M3, "xt0%d" % h) for h in range(2)])
        w10 = weave_dz(1, 0, True)
        t = turn(go_rows[1], empty_dz)
        dz_t.append([quantize(t[h], E5M2, "dzt1%d" % h) for h in range(2)])
        t = turn(x_rows[1], empty_x)
        w11 = weave_dz(1, 1, True)
        dz_m[0].append(quantize(w00, E5M2, "dzm00"))
        dz_m[1].append(quantize(w01, E5M2, "dzm01"))
        x_t.append([quantize(t[h], E4M3, "xt1%d" % h) for h in range(2)])
        dz_m[0].append(quantize(w10, E5M2, "dzm10"))
        dz_m[1].append(quantize(w11, E5M2, "dzm11"))
        out1_block(0, 0)
        out1_block(1, 0)
        out1_block(0, 1)
        out1_block(1, 1)

        parts = N // BLEND_COLS
        steps = [(g, part) for part in range(parts) for g in range(2)]
        blend = [[] for part in range(parts)]
        groups = [(b, half) for b in range(2) for half in range(2)]
        open_sums = {}

        def open_part(part):
            for b, half in groups:
                open_sums[(part, b, half)] = banks.tile([P, BANK], F32, name="bank")
                one_pass(open_sums[(part, b, half)], blend[part], b * P, dz_m[half], 0)

        def close_part(part):
            dx = results.tile([P, 2, D], F32, name="result")
            for b, half in groups:
                acc = open_sums[(part, b, half)]
                one_pass(acc, blend[part], b * P, dz_m[half], 1)
                dst = dx[:, b, half * BANK : (half + 1) * BANK]
                if part == parts - 1 and half == 1:
                    nc.vector.tensor_scalar(out=dst, in0=acc[:], scalar1=HALF, scalar2=None, op0=MULT)
                else:
                    nc.scalar.activation(out=dst, in_=acc[:], func=COPY, scale=HALF)
            rows = out_0[part * BLEND_COLS : (part + 1) * BLEND_COLS, :]
            nc.sync.dma_start(out=rows.rearrange("(b p) d -> p b d", p=P), in_=dx[:])

        waiting = weave_sum(*steps[0])
        for s, (g, part) in enumerate(steps):
            ready = waiting
            if s + 1 < len(steps):
                waiting = weave_sum(*steps[s + 1])
            blend[part].append(quantize(ready, E4M3, "blend%d%d" % (g, part)))
            if g == 0:
                open_part(part)
            else:
                close_part(part)
